import numpy as np
import ml_dtypes


def mxq(x, axis, fmt="e4m3"):
    dtype, down = {"e4m3": (ml_dtypes.float8_e4m3fn, 7), "e5m2": (ml_dtypes.float8_e5m2, 14)}[fmt]
    v = np.moveaxis(np.asarray(x, np.float32).astype(ml_dtypes.bfloat16).astype(np.float64), axis, -1)
    blocks = v.reshape(v.shape[:-1] + (-1, 32))
    amax = np.abs(blocks).max(-1, keepdims=True)
    byte = np.maximum(np.where(amax > 0, np.frexp(amax)[1] - 1 + 127, 0) - down, 1)
    scale = np.exp2(byte - 127.0)
    codes = (blocks / scale).astype(np.float32).astype(dtype).astype(np.float64)
    return np.moveaxis((codes * scale).reshape(v.shape), -1, axis)


WIDE = False


def mx_kscale(k):
    if not WIDE:
        return np.ones(k)
    levels = np.array([10, -10, 5, -5, 0])
    a = np.random.permutation(np.resize(levels, k // 512 * 4)).reshape(k // 512, 4)
    idx = np.arange(k)
    return np.exp2(a[idx // 512, idx % 128 // 32])


BF16 = ml_dtypes.bfloat16


def bf(x):
    return np.asarray(x, np.float32).astype(BF16)


def f64(x):
    return np.asarray(x).astype(np.float64)


B, S, H, HD = 4, 2048, 4, 128
DIM = H * HD


def setup_inputs():
    s, t = mx_kscale(DIM), mx_kscale(DIM)
    return {"x": bf(np.random.standard_normal((B, S, DIM)) * 2.0 * s),
            "y_norm": bf(np.random.standard_normal((B, S, DIM))),
            "wg_w": bf(np.random.standard_normal((DIM, DIM)) * 0.5 / np.sqrt(DIM) / s[:, None] * t),
            "wo_w": bf(np.random.standard_normal((DIM, DIM)) * 1.5 / np.sqrt(DIM) / t[:, None])}


def reference(x, y_norm, wg_w, wo_w):
    g = np.maximum(mxq(f64(x), 2, "e4m3") @ mxq(f64(wg_w), 0, "e4m3"), 0.0)
    h = g * f64(y_norm)
    return mxq(h, 2, "e4m3") @ mxq(f64(wo_w), 0, "e4m3")

@@ -1,0 +1,227 @@
+from contextlib import ExitStack
+
+import concourse.mybir as mybir
+from concourse.masks import make_identity
+
+BF16 = mybir.dt.bfloat16
+F32 = mybir.dt.float32
+U32 = mybir.dt.uint32
+U8 = mybir.dt.uint8
+FP8X4 = mybir.dt.float8_e4m3fn_x4
+
+P = 128
+PACK = 4
+D = P * PACK
+WORDS = D // 2
+TOKENS = 4 * 2048
+
+SUBS = 8
+CHUNK = SUBS * P
+CHUNKS = TOKENS // CHUNK
+ROUND_SUBS = 2
+ROUNDS = TOKENS // (ROUND_SUBS * P)
+CHUNK_ROUNDS = SUBS // ROUND_SUBS
+STORE_ROUNDS = 2
+LOADS_AHEAD = 3
+
+FIRST_MATMUL_LAG = 1
+QUANTISE_H_LAG = 2
+SECOND_MATMUL_LAG = 3
+
+VECTOR_OUT_SHARE = 4
+
+FLOPS = 2 * 2 * TOKENS * D * D
+
+
+def tile_multiscaleretention_pb_t_kernel(tc, x, y_norm, wg_w, wo_w, out):
+    nc = tc.nc
+    x_rows = x.flatten_outer_dims()
+    y_rows = y_norm.flatten_outer_dims()
+    out_rows = out.flatten_outer_dims()
+
+    def chunk_view(rows, c):
+        return rows[c * CHUNK : (c + 1) * CHUNK, :].rearrange("(p s) d -> p (s d)", s=SUBS)
+
+    with ExitStack() as ctx:
+        ctx.enter_context(tc.manual_schedule())
+        const = ctx.enter_context(tc.tile_pool(name="const", bufs=1))
+        loads = ctx.enter_context(tc.tile_pool(name="loads", bufs=LOADS_AHEAD + 1))
+        work = ctx.enter_context(tc.tile_pool(name="work", bufs=3))
+        stores = ctx.enter_context(tc.tile_pool(name="stores", bufs=4))
+        psum = ctx.enter_context(tc.psum_pool(name="psum", bufs=2))
+
+        x_chunks = {}
+        y_chunks = {}
+
+        def new_chunk(c):
+            x_sb = loads.tile([P, SUBS * D], BF16, tag="x")
+            y_sb = loads.tile([P, SUBS * D], BF16, tag="y")
+            x_chunks[c] = x_sb
+            y_chunks[c] = y_sb
+
+        def load_rounds(c, first_round, rounds):
+            cols = slice(first_round * ROUND_SUBS * D, (first_round + rounds) * ROUND_SUBS * D)
+            nc.sync.dma_start(out=x_chunks[c][:, cols], in_=chunk_view(x_rows, c)[:, cols])
+            nc.sync.dma_start(out=y_chunks[c][:, cols], in_=chunk_view(y_rows, c)[:, cols])
+
+        def load_chunk(c):
+            new_chunk(c)
+            load_rounds(c, 0, CHUNK_ROUNDS)
+
+        def load_weight(w, name):
+            raw = const.tile([P, 2, 2 * D], BF16, name=name)
+            nc.sync.dma_start(out=raw[:], in_=w.rearrange("(u p e) c -> p u (e c)", u=2, e=2))
+            return raw
+
+        wg_raw = load_weight(wg_w, "wg_raw")
+        new_chunk(0)
+        load_rounds(0, 0, 1)
+        wo_raw = load_weight(wo_w, "wo_raw")
+        for r in range(1, CHUNK_ROUNDS):
+            load_rounds(0, r, 1)
+        for c in range(1, LOADS_AHEAD):
+            load_chunk(c)
+
+        ident = const.tile([P, P], F32)
+        make_identity(nc, ident[:])
+
+        def quantise_weight(grouped, name):
+            codes = const.tile([P, D], U32, name=name + "_codes", align_bytes=64)
+            scales = const.tile([P, D], U8, name=name + "_scales", align_bytes=64)
+            nc.vector.quantize_mx(out=codes[:].bitcast(FP8X4), scales=scales[:], in_=grouped[:])
+            return codes, scales
+
+        wg_grouped = const.tile([P, D * PACK], BF16, align_bytes=64)
+        wg_sorted = wg_grouped[:].rearrange("p (u e q t) -> p u e q t", u=2, e=2, t=PACK)
+        wg_rows = wg_raw[:].rearrange("p a (b c) -> p (a b) c", b=2)
+        wg_cols = wg_rows.rearrange("p t (u q e) -> p u e q t", u=2, e=2)
+        for u in range(2):
+            for e in range(2):
+                nc.vector.tensor_copy(out=wg_sorted[:, u, e], in_=wg_cols[:, u, e])
+        wg_codes, wg_scales = quantise_weight(wg_grouped, "wg")
+
+        wo_mx = {}
+
+        def prepare_wo():
+            wo_grouped = const.tile([P, D * PACK], BF16, align_bytes=64)
+            nc.vector.tensor_copy(
+                out=wo_grouped[:].rearrange("p (c t) -> p c t", t=PACK),
+                in_=wo_raw[:].rearrange("p a (b c) -> p c (a b)", b=2),
+            )
+            wo_mx["codes"], wo_mx["scales"] = quantise_weight(wo_grouped, "wo")
+
+        x_mx = {}
+        y_grouped = {}
+        h_grouped = {}
+        h_mx = {}
+        out_tiles = {}
+
+        def transpose_round(r):
+            c, first_sub = r // CHUNK_ROUNDS, (r % CHUNK_ROUNDS) * ROUND_SUBS
+            banks = []
+            for chunks, tag in ((x_chunks, "xT"), (y_chunks, "yT")):
+                words = chunks[c][:].bitcast(F32)
+                bank = psum.tile([P, ROUND_SUBS, 2, P], F32, tag=tag)
+                for s in range(ROUND_SUBS):
+                    for u in range(2):
+                        start = (first_sub + s) * WORDS + u * P
+                        nc.tensor.transpose(bank[:, s, u, :], words[:, start : start + P], ident[:])
+                banks.append(bank)
+            grouped = []
+            for bank, tag in zip(banks, ("x_grouped", "y_grouped")):
+                tile_bf16 = work.tile([P, ROUND_SUBS * D], BF16, tag=tag, align_bytes=64)
+                nc.scalar.copy(
+                    out=tile_bf16[:].bitcast(F32).rearrange("p (s r u) -> p s r u", s=ROUND_SUBS, u=2),
+                    in_=bank[:].rearrange("p s u r -> p s r u"),
+                )
+                grouped.append(tile_bf16)
+            y_grouped[r] = grouped[1]
+            x_mx[r] = quantise_round(grouped[0], "x")
+
+        def quantise_round(grouped, name):
+            codes = work.tile([P, ROUND_SUBS * P], U32, tag=name + "_codes", align_bytes=64)
+            scales = work.tile([P, ROUND_SUBS * P], U8, tag=name + "_scales", align_bytes=64)
+            nc.vector.quantize_mx(out=codes[:].bitcast(FP8X4), scales=scales[:], in_=grouped[:])
+            return codes, scales
+
+        def first_matmul_round(r):
+            codes, scales = x_mx[r]
+            y_bf16 = y_grouped[r]
+            h_bf16 = work.tile([P, ROUND_SUBS * D], BF16, tag="h_grouped", align_bytes=64)
+            g_banks = []
+            for s in range(ROUND_SUBS):
+                tokens = slice(s * P, (s + 1) * P)
+                g_bank = psum.tile([P, PACK, P], F32, tag="g")
+                for t in range(PACK):
+                    cols = slice(t * P, (t + 1) * P)
+                    nc.tensor.matmul_mx(
+                        out=g_bank[:, t, :],
+                        lhsT=wg_codes[:, cols].bitcast(FP8X4),
+                        lhsT_scale=wg_scales[:, cols],
+                        rhs=codes[:, tokens].bitcast(FP8X4),
+                        rhs_scale=scales[:, tokens],
+                        start=True,
+                        stop=True,
+                    )
+                g_banks.append(g_bank)
+            for s in range(ROUND_SUBS):
+                span = slice(s * D, (s + 1) * D)
+                nc.vector.scalar_tensor_tensor(
+                    out=h_bf16[:, span].rearrange("p (r t) -> p r t", t=PACK),
+                    in0=g_banks[s][:].rearrange("p t r -> p r t"),
+                    scalar=0.0,
+                    in1=y_bf16[:, span].rearrange("p (r t) -> p r t", t=PACK),
+                    op0=mybir.AluOpType.max,
+                    op1=mybir.AluOpType.mult,
+                )
+            h_grouped[r] = h_bf16
+
+        def second_matmul_round(r):
+            codes, scales = h_mx[r]
+            if r % STORE_ROUNDS == 0:
+                out_sb = stores.tile([P, STORE_ROUNDS * ROUND_SUBS * D], F32)
+                out_tiles[r // STORE_ROUNDS] = out_sb
+            out_sb = out_tiles[r // STORE_ROUNDS]
+            out_banks = []
+            for s in range(ROUND_SUBS):
+                tokens = slice(s * P, (s + 1) * P)
+                out_bank = psum.tile([P, D], F32, tag="out")
+                nc.tensor.matmul_mx(
+                    out=out_bank[:],
+                    lhsT=codes[:, tokens].bitcast(FP8X4),
+                    lhsT_scale=scales[:, tokens],
+                    rhs=wo_mx["codes"][:].bitcast(FP8X4),
+                    rhs_scale=wo_mx["scales"][:],
+                    start=True,
+                    stop=True,
+                )
+                out_banks.append(out_bank)
+            for s in range(ROUND_SUBS):
+                sub = (r % STORE_ROUNDS) * ROUND_SUBS + s
+                span = slice(sub * D, (sub + 1) * D)
+                if (r * ROUND_SUBS + s) % VECTOR_OUT_SHARE == VECTOR_OUT_SHARE - 1:
+                    nc.vector.tensor_copy(out=out_sb[:, span], in_=out_banks[s][:])
+                else:
+                    nc.scalar.copy(out=out_sb[:, span], in_=out_banks[s][:])
+            if r % STORE_ROUNDS == STORE_ROUNDS - 1:
+                c = r // CHUNK_ROUNDS
+                width = STORE_ROUNDS * ROUND_SUBS * D
+                first = (r % CHUNK_ROUNDS - (STORE_ROUNDS - 1)) * ROUND_SUBS * D
+                nc.sync.dma_start(
+                    out=chunk_view(out_rows, c)[:, first : first + width],
+                    in_=out_sb[:],
+                )
+
+        for i in range(ROUNDS + SECOND_MATMUL_LAG):
+            if i % CHUNK_ROUNDS == 0 and i // CHUNK_ROUNDS + LOADS_AHEAD < CHUNKS:
+                load_chunk(i // CHUNK_ROUNDS + LOADS_AHEAD)
+            if i < ROUNDS:
+                transpose_round(i)
+            if i == 0:
+                prepare_wo()
+            if 0 <= i - QUANTISE_H_LAG < ROUNDS:
+                h_mx[i - QUANTISE_H_LAG] = quantise_round(h_grouped[i - QUANTISE_H_LAG], "h")
+            if 0 <= i - FIRST_MATMUL_LAG < ROUNDS:
+                first_matmul_round(i - FIRST_MATMUL_LAG)
+            if 0 <= i - SECOND_MATMUL_LAG < ROUNDS:
+                second_matmul_round(i - SECOND_MATMUL_LAG)

@@ -19,16 +19,16 @@ SUBS = 8
 CHUNK = SUBS * P
 CHUNKS = TOKENS // CHUNK
 ROUND_SUBS = 2
+ROUND_COLS = ROUND_SUBS * D
 ROUNDS = TOKENS // (ROUND_SUBS * P)
 CHUNK_ROUNDS = SUBS // ROUND_SUBS
-STORE_ROUNDS = 2
 LOADS_AHEAD = 3
 
 FIRST_MATMUL_LAG = 1
 QUANTISE_H_LAG = 2
 SECOND_MATMUL_LAG = 3
 
-VECTOR_OUT_SHARE = 4
+VECTOR_OUT_SHARE = 8
 
 FLOPS = 2 * 2 * TOKENS * D * D
 
@@ -47,39 +47,38 @@ def tile_multiscaleretention_pb_t_kernel(tc, x, y_norm, wg_w, wo_w, out):
         const = ctx.enter_context(tc.tile_pool(name="const", bufs=1))
         loads = ctx.enter_context(tc.tile_pool(name="loads", bufs=LOADS_AHEAD + 1))
         work = ctx.enter_context(tc.tile_pool(name="work", bufs=3))
-        stores = ctx.enter_context(tc.tile_pool(name="stores", bufs=4))
-        psum = ctx.enter_context(tc.psum_pool(name="psum", bufs=2))
+        stores = ctx.enter_context(tc.tile_pool(name="stores", bufs=10))
+        psum_t = ctx.enter_context(tc.psum_pool(name="psum_t", bufs=1))
+        psum_mx = ctx.enter_context(tc.psum_pool(name="psum_mx", bufs=3))
 
         x_chunks = {}
         y_chunks = {}
 
-        def new_chunk(c):
-            x_sb = loads.tile([P, SUBS * D], BF16, tag="x")
-            y_sb = loads.tile([P, SUBS * D], BF16, tag="y")
-            x_chunks[c] = x_sb
-            y_chunks[c] = y_sb
-
         def load_rounds(c, first_round, rounds):
-            cols = slice(first_round * ROUND_SUBS * D, (first_round + rounds) * ROUND_SUBS * D)
+            cols = slice(first_round * ROUND_COLS, (first_round + rounds) * ROUND_COLS)
             nc.sync.dma_start(out=x_chunks[c][:, cols], in_=chunk_view(x_rows, c)[:, cols])
             nc.sync.dma_start(out=y_chunks[c][:, cols], in_=chunk_view(y_rows, c)[:, cols])
-
-        def load_chunk(c):
-            new_chunk(c)
-            load_rounds(c, 0, CHUNK_ROUNDS)
 
         def load_weight(w, name):
             raw = const.tile([P, 2, 2 * D], BF16, name=name)
             nc.sync.dma_start(out=raw[:], in_=w.rearrange("(u p e) c -> p u (e c)", u=2, e=2))
             return raw
 
-        wg_raw = load_weight(wg_w, "wg_raw")
-        new_chunk(0)
-        load_rounds(0, 0, 1)
-        wo_raw = load_weight(wo_w, "wo_raw")
-        for r in range(1, CHUNK_ROUNDS):
-            load_rounds(0, r, 1)
-        for c in range(1, LOADS_AHEAD):
+        weights_raw = {}
+
+        def load_chunk(c):
+            x_sb = loads.tile([P, SUBS * D], BF16, tag="x")
+            y_sb = loads.tile([P, SUBS * D], BF16, tag="y")
+            x_chunks[c] = x_sb
+            y_chunks[c] = y_sb
+            rounds = min(CHUNK_ROUNDS, 2**c)
+            for first_round in range(0, CHUNK_ROUNDS, rounds):
+                load_rounds(c, first_round, rounds)
+                if c == 0 and first_round == 0:
+                    weights_raw["wo"] = load_weight(wo_w, "wo_raw")
+
+        weights_raw["wg"] = load_weight(wg_w, "wg_raw")
+        for c in range(LOADS_AHEAD):
             load_chunk(c)
 
         ident = const.tile([P, P], F32)
@@ -93,7 +92,7 @@ def tile_multiscaleretention_pb_t_kernel(tc, x, y_norm, wg_w, wo_w, out):
 
         wg_grouped = const.tile([P, D * PACK], BF16, align_bytes=64)
         wg_sorted = wg_grouped[:].rearrange("p (u e q t) -> p u e q t", u=2, e=2, t=PACK)
-        wg_rows = wg_raw[:].rearrange("p a (b c) -> p (a b) c", b=2)
+        wg_rows = weights_raw["wg"][:].rearrange("p a (b c) -> p (a b) c", b=2)
         wg_cols = wg_rows.rearrange("p t (u q e) -> p u e q t", u=2, e=2)
         for u in range(2):
             for e in range(2):
@@ -106,37 +105,36 @@ def tile_multiscaleretention_pb_t_kernel(tc, x, y_norm, wg_w, wo_w, out):
             wo_grouped = const.tile([P, D * PACK], BF16, align_bytes=64)
             nc.vector.tensor_copy(
                 out=wo_grouped[:].rearrange("p (c t) -> p c t", t=PACK),
-                in_=wo_raw[:].rearrange("p a (b c) -> p c (a b)", b=2),
+                in_=weights_raw["wo"][:].rearrange("p a (b c) -> p c (a b)", b=2),
             )
             wo_mx["codes"], wo_mx["scales"] = quantise_weight(wo_grouped, "wo")
 
-        x_mx = {}
+        x_grouped = {}
         y_grouped = {}
+        x_mx = {}
+        g_banks = {}
         h_grouped = {}
         h_mx = {}
-        out_tiles = {}
+        out_banks = {}
 
         def transpose_round(r):
             c, first_sub = r // CHUNK_ROUNDS, (r % CHUNK_ROUNDS) * ROUND_SUBS
             banks = []
             for chunks, tag in ((x_chunks, "xT"), (y_chunks, "yT")):
                 words = chunks[c][:].bitcast(F32)
-                bank = psum.tile([P, ROUND_SUBS, 2, P], F32, tag=tag)
+                bank = psum_t.tile([P, ROUND_SUBS, 2, P], F32, tag=tag)
                 for s in range(ROUND_SUBS):
                     for u in range(2):
                         start = (first_sub + s) * WORDS + u * P
                         nc.tensor.transpose(bank[:, s, u, :], words[:, start : start + P], ident[:])
                 banks.append(bank)
-            grouped = []
-            for bank, tag in zip(banks, ("x_grouped", "y_grouped")):
-                tile_bf16 = work.tile([P, ROUND_SUBS * D], BF16, tag=tag, align_bytes=64)
+            for bank, grouped, tag in zip(banks, (x_grouped, y_grouped), ("x_grouped", "y_grouped")):
+                tile_bf16 = work.tile([P, ROUND_COLS], BF16, tag=tag, align_bytes=64)
                 nc.scalar.copy(
                     out=tile_bf16[:].bitcast(F32).rearrange("p (s r u) -> p s r u", s=ROUND_SUBS, u=2),
                     in_=bank[:].rearrange("p s u r -> p s r u"),
                 )
-                grouped.append(tile_bf16)
-            y_grouped[r] = grouped[1]
-            x_mx[r] = quantise_round(grouped[0], "x")
+                grouped[r] = tile_bf16
 
         def quantise_round(grouped, name):
             codes = work.tile([P, ROUND_SUBS * P], U32, tag=name + "_codes", align_bytes=64)
@@ -146,12 +144,10 @@ def tile_multiscaleretention_pb_t_kernel(tc, x, y_norm, wg_w, wo_w, out):
 
         def first_matmul_round(r):
             codes, scales = x_mx[r]
-            y_bf16 = y_grouped[r]
-            h_bf16 = work.tile([P, ROUND_SUBS * D], BF16, tag="h_grouped", align_bytes=64)
-            g_banks = []
+            g_banks[r] = []
             for s in range(ROUND_SUBS):
                 tokens = slice(s * P, (s + 1) * P)
-                g_bank = psum.tile([P, PACK, P], F32, tag="g")
+                g_bank = psum_mx.tile([P, PACK, P], F32, tag="g")
                 for t in range(PACK):
                     cols = slice(t * P, (t + 1) * P)
                     nc.tensor.matmul_mx(
@@ -163,14 +159,17 @@ def tile_multiscaleretention_pb_t_kernel(tc, x, y_norm, wg_w, wo_w, out):
                         start=True,
                         stop=True,
                     )
-                g_banks.append(g_bank)
+                g_banks[r].append(g_bank)
+
+        def gate_round(r):
+            h_bf16 = work.tile([P, ROUND_COLS], BF16, tag="h_grouped", align_bytes=64)
             for s in range(ROUND_SUBS):
                 span = slice(s * D, (s + 1) * D)
                 nc.vector.scalar_tensor_tensor(
                     out=h_bf16[:, span].rearrange("p (r t) -> p r t", t=PACK),
-                    in0=g_banks[s][:].rearrange("p t r -> p r t"),
+                    in0=g_banks[r][s][:].rearrange("p t r -> p r t"),
                     scalar=0.0,
-                    in1=y_bf16[:, span].rearrange("p (r t) -> p r t", t=PACK),
+                    in1=y_grouped[r][:, span].rearrange("p (r t) -> p r t", t=PACK),
                     op0=mybir.AluOpType.max,
                     op1=mybir.AluOpType.mult,
                 )
@@ -178,14 +177,10 @@ def tile_multiscaleretention_pb_t_kernel(tc, x, y_norm, wg_w, wo_w, out):
 
         def second_matmul_round(r):
             codes, scales = h_mx[r]
-            if r % STORE_ROUNDS == 0:
-                out_sb = stores.tile([P, STORE_ROUNDS * ROUND_SUBS * D], F32)
-                out_tiles[r // STORE_ROUNDS] = out_sb
-            out_sb = out_tiles[r // STORE_ROUNDS]
-            out_banks = []
+            out_banks[r] = []
             for s in range(ROUND_SUBS):
                 tokens = slice(s * P, (s + 1) * P)
-                out_bank = psum.tile([P, D], F32, tag="out")
+                out_bank = psum_mx.tile([P, D], F32, tag="out")
                 nc.tensor.matmul_mx(
                     out=out_bank[:],
                     lhsT=codes[:, tokens].bitcast(FP8X4),
@@ -195,33 +190,37 @@ def tile_multiscaleretention_pb_t_kernel(tc, x, y_norm, wg_w, wo_w, out):
                     start=True,
                     stop=True,
                 )
-                out_banks.append(out_bank)
+                out_banks[r].append(out_bank)
+
+        def store_round(r):
+            out_sb = stores.tile([P, ROUND_COLS], F32)
             for s in range(ROUND_SUBS):
-                sub = (r % STORE_ROUNDS) * ROUND_SUBS + s
-                span = slice(sub * D, (sub + 1) * D)
+                span = slice(s * D, (s + 1) * D)
                 if (r * ROUND_SUBS + s) % VECTOR_OUT_SHARE == VECTOR_OUT_SHARE - 1:
-                    nc.vector.tensor_copy(out=out_sb[:, span], in_=out_banks[s][:])
+                    nc.vector.tensor_copy(out=out_sb[:, span], in_=out_banks[r][s][:])
                 else:
-                    nc.scalar.copy(out=out_sb[:, span], in_=out_banks[s][:])
-            if r % STORE_ROUNDS == STORE_ROUNDS - 1:
-                c = r // CHUNK_ROUNDS
-                width = STORE_ROUNDS * ROUND_SUBS * D
-                first = (r % CHUNK_ROUNDS - (STORE_ROUNDS - 1)) * ROUND_SUBS * D
-                nc.sync.dma_start(
-                    out=chunk_view(out_rows, c)[:, first : first + width],
-                    in_=out_sb[:],
-                )
+                    nc.scalar.copy(out=out_sb[:, span], in_=out_banks[r][s][:])
+            first = (r % CHUNK_ROUNDS) * ROUND_COLS
+            nc.sync.dma_start(
+                out=chunk_view(out_rows, r // CHUNK_ROUNDS)[:, first : first + ROUND_COLS],
+                in_=out_sb[:],
+            )
 
         for i in range(ROUNDS + SECOND_MATMUL_LAG):
             if i % CHUNK_ROUNDS == 0 and i // CHUNK_ROUNDS + LOADS_AHEAD < CHUNKS:
                 load_chunk(i // CHUNK_ROUNDS + LOADS_AHEAD)
             if i < ROUNDS:
                 transpose_round(i)
+                x_mx[i] = quantise_round(x_grouped[i], "x")
             if i == 0:
                 prepare_wo()
             if 0 <= i - QUANTISE_H_LAG < ROUNDS:
                 h_mx[i - QUANTISE_H_LAG] = quantise_round(h_grouped[i - QUANTISE_H_LAG], "h")
+            if 0 <= i - SECOND_MATMUL_LAG < ROUNDS:
+                second_matmul_round(i - SECOND_MATMUL_LAG)
             if 0 <= i - FIRST_MATMUL_LAG < ROUNDS:
                 first_matmul_round(i - FIRST_MATMUL_LAG)
             if 0 <= i - SECOND_MATMUL_LAG < ROUNDS:
-                second_matmul_round(i - SECOND_MATMUL_LAG)
+                store_round(i - SECOND_MATMUL_LAG)
+            if 0 <= i - FIRST_MATMUL_LAG < ROUNDS:
+                gate_round(i - FIRST_MATMUL_LAG)

@@ -43,7 +43,6 @@ def tile_multiscaleretention_pb_t_kernel(tc, x, y_norm, wg_w, wo_w, out):
         return rows[c * CHUNK : (c + 1) * CHUNK, :].rearrange("(p s) d -> p (s d)", s=SUBS)
 
     with ExitStack() as ctx:
-        ctx.enter_context(tc.manual_schedule())
         const = ctx.enter_context(tc.tile_pool(name="const", bufs=1))
         loads = ctx.enter_context(tc.tile_pool(name="loads", bufs=LOADS_AHEAD + 1))
         work = ctx.enter_context(tc.tile_pool(name="work", bufs=3))

from contextlib import ExitStack

import concourse.mybir as mybir
from concourse.masks import make_identity

BF16 = mybir.dt.bfloat16
F32 = mybir.dt.float32
U32 = mybir.dt.uint32
U8 = mybir.dt.uint8
FP8X4 = mybir.dt.float8_e4m3fn_x4

P = 128
PACK = 4
D = P * PACK
WORDS = D // 2
TOKENS = 4 * 2048

SUBS = 8
CHUNK = SUBS * P
CHUNKS = TOKENS // CHUNK
ROUND_SUBS = 2
ROUND_COLS = ROUND_SUBS * D
ROUNDS = TOKENS // (ROUND_SUBS * P)
CHUNK_ROUNDS = SUBS // ROUND_SUBS
LOADS_AHEAD = 3

FIRST_MATMUL_LAG = 1
QUANTISE_H_LAG = 2
SECOND_MATMUL_LAG = 3

VECTOR_OUT_SHARE = 8

FLOPS = 2 * 2 * TOKENS * D * D


def tile_multiscaleretention_pb_t_kernel(tc, x, y_norm, wg_w, wo_w, out):
    nc = tc.nc
    x_rows = x.flatten_outer_dims()
    y_rows = y_norm.flatten_outer_dims()
    out_rows = out.flatten_outer_dims()

    def chunk_view(rows, c):
        return rows[c * CHUNK : (c + 1) * CHUNK, :].rearrange("(p s) d -> p (s d)", s=SUBS)

    with ExitStack() as ctx:
        const = ctx.enter_context(tc.tile_pool(name="const", bufs=1))
        loads = ctx.enter_context(tc.tile_pool(name="loads", bufs=LOADS_AHEAD + 1))
        work = ctx.enter_context(tc.tile_pool(name="work", bufs=3))
        stores = ctx.enter_context(tc.tile_pool(name="stores", bufs=10))
        psum_t = ctx.enter_context(tc.psum_pool(name="psum_t", bufs=1))
        psum_mx = ctx.enter_context(tc.psum_pool(name="psum_mx", bufs=3))

        x_chunks = {}
        y_chunks = {}

        def load_rounds(c, first_round, rounds):
            cols = slice(first_round * ROUND_COLS, (first_round + rounds) * ROUND_COLS)
            nc.sync.dma_start(out=x_chunks[c][:, cols], in_=chunk_view(x_rows, c)[:, cols])
            nc.sync.dma_start(out=y_chunks[c][:, cols], in_=chunk_view(y_rows, c)[:, cols])

        def load_weight(w, name):
            raw = const.tile([P, 2, 2 * D], BF16, name=name)
            nc.sync.dma_start(out=raw[:], in_=w.rearrange("(u p e) c -> p u (e c)", u=2, e=2))
            return raw

        weights_raw = {}

        def load_chunk(c):
            x_sb = loads.tile([P, SUBS * D], BF16, tag="x")
            y_sb = loads.tile([P, SUBS * D], BF16, tag="y")
            x_chunks[c] = x_sb
            y_chunks[c] = y_sb
            rounds = min(CHUNK_ROUNDS, 2**c)
            for first_round in range(0, CHUNK_ROUNDS, rounds):
                load_rounds(c, first_round, rounds)
                if c == 0 and first_round == 0:
                    weights_raw["wo"] = load_weight(wo_w, "wo_raw")

        weights_raw["wg"] = load_weight(wg_w, "wg_raw")
        for c in range(LOADS_AHEAD):
            load_chunk(c)

        ident = const.tile([P, P], F32)
        make_identity(nc, ident[:])

        def quantise_weight(grouped, name):
            codes = const.tile([P, D], U32, name=name + "_codes", align_bytes=64)
            scales = const.tile([P, D], U8, name=name + "_scales", align_bytes=64)
            nc.vector.quantize_mx(out=codes[:].bitcast(FP8X4), scales=scales[:], in_=grouped[:])
            return codes, scales

        wg_grouped = const.tile([P, D * PACK], BF16, align_bytes=64)
        wg_sorted = wg_grouped[:].rearrange("p (u e q t) -> p u e q t", u=2, e=2, t=PACK)
        wg_rows = weights_raw["wg"][:].rearrange("p a (b c) -> p (a b) c", b=2)
        wg_cols = wg_rows.rearrange("p t (u q e) -> p u e q t", u=2, e=2)
        for u in range(2):
            for e in range(2):
                nc.vector.tensor_copy(out=wg_sorted[:, u, e], in_=wg_cols[:, u, e])
        wg_codes, wg_scales = quantise_weight(wg_grouped, "wg")

        wo_mx = {}

        def prepare_wo():
            wo_grouped = const.tile([P, D * PACK], BF16, align_bytes=64)
            nc.vector.tensor_copy(
                out=wo_grouped[:].rearrange("p (c t) -> p c t", t=PACK),
                in_=weights_raw["wo"][:].rearrange("p a (b c) -> p c (a b)", b=2),
            )
            wo_mx["codes"], wo_mx["scales"] = quantise_weight(wo_grouped, "wo")

        x_grouped = {}
        y_grouped = {}
        x_mx = {}
        g_banks = {}
        h_grouped = {}
        h_mx = {}
        out_banks = {}

        def transpose_round(r):
            c, first_sub = r // CHUNK_ROUNDS, (r % CHUNK_ROUNDS) * ROUND_SUBS
            banks = []
            for chunks, tag in ((x_chunks, "xT"), (y_chunks, "yT")):
                words = chunks[c][:].bitcast(F32)
                bank = psum_t.tile([P, ROUND_SUBS, 2, P], F32, tag=tag)
                for s in range(ROUND_SUBS):
                    for u in range(2):
                        start = (first_sub + s) * WORDS + u * P
                        nc.tensor.transpose(bank[:, s, u, :], words[:, start : start + P], ident[:])
                banks.append(bank)
            for bank, grouped, tag in zip(banks, (x_grouped, y_grouped), ("x_grouped", "y_grouped")):
                tile_bf16 = work.tile([P, ROUND_COLS], BF16, tag=tag, align_bytes=64)
                nc.scalar.copy(
                    out=tile_bf16[:].bitcast(F32).rearrange("p (s r u) -> p s r u", s=ROUND_SUBS, u=2),
                    in_=bank[:].rearrange("p s u r -> p s r u"),
                )
                grouped[r] = tile_bf16

        def quantise_round(grouped, name):
            codes = work.tile([P, ROUND_SUBS * P], U32, tag=name + "_codes", align_bytes=64)
            scales = work.tile([P, ROUND_SUBS * P], U8, tag=name + "_scales", align_bytes=64)
            nc.vector.quantize_mx(out=codes[:].bitcast(FP8X4), scales=scales[:], in_=grouped[:])
            return codes, scales

        def first_matmul_round(r):
            codes, scales = x_mx[r]
            g_banks[r] = []
            for s in range(ROUND_SUBS):
                tokens = slice(s * P, (s + 1) * P)
                g_bank = psum_mx.tile([P, PACK, P], F32, tag="g")
                for t in range(PACK):
                    cols = slice(t * P, (t + 1) * P)
                    nc.tensor.matmul_mx(
                        out=g_bank[:, t, :],
                        lhsT=wg_codes[:, cols].bitcast(FP8X4),
                        lhsT_scale=wg_scales[:, cols],
                        rhs=codes[:, tokens].bitcast(FP8X4),
                        rhs_scale=scales[:, tokens],
                        start=True,
                        stop=True,
                    )
                g_banks[r].append(g_bank)

        def gate_round(r):
            h_bf16 = work.tile([P, ROUND_COLS], BF16, tag="h_grouped", align_bytes=64)
            for s in range(ROUND_SUBS):
                span = slice(s * D, (s + 1) * D)
                nc.vector.scalar_tensor_tensor(
                    out=h_bf16[:, span].rearrange("p (r t) -> p r t", t=PACK),
                    in0=g_banks[r][s][:].rearrange("p t r -> p r t"),
                    scalar=0.0,
                    in1=y_grouped[r][:, span].rearrange("p (r t) -> p r t", t=PACK),
                    op0=mybir.AluOpType.max,
                    op1=mybir.AluOpType.mult,
                )
            h_grouped[r] = h_bf16

        def second_matmul_round(r):
            codes, scales = h_mx[r]
            out_banks[r] = []
            for s in range(ROUND_SUBS):
                tokens = slice(s * P, (s + 1) * P)
                out_bank = psum_mx.tile([P, D], F32, tag="out")
                nc.tensor.matmul_mx(
                    out=out_bank[:],
                    lhsT=codes[:, tokens].bitcast(FP8X4),
                    lhsT_scale=scales[:, tokens],
                    rhs=wo_mx["codes"][:].bitcast(FP8X4),
                    rhs_scale=wo_mx["scales"][:],
                    start=True,
                    stop=True,
                )
                out_banks[r].append(out_bank)

        def store_round(r):
            out_sb = stores.tile([P, ROUND_COLS], F32)
            for s in range(ROUND_SUBS):
                span = slice(s * D, (s + 1) * D)
                if (r * ROUND_SUBS + s) % VECTOR_OUT_SHARE == VECTOR_OUT_SHARE - 1:
                    nc.vector.tensor_copy(out=out_sb[:, span], in_=out_banks[r][s][:])
                else:
                    nc.scalar.copy(out=out_sb[:, span], in_=out_banks[r][s][:])
            first = (r % CHUNK_ROUNDS) * ROUND_COLS
            nc.sync.dma_start(
                out=chunk_view(out_rows, r // CHUNK_ROUNDS)[:, first : first + ROUND_COLS],
                in_=out_sb[:],
            )

        for i in range(ROUNDS + SECOND_MATMUL_LAG):
            if i % CHUNK_ROUNDS == 0 and i // CHUNK_ROUNDS + LOADS_AHEAD < CHUNKS:
                load_chunk(i // CHUNK_ROUNDS + LOADS_AHEAD)
            if i < ROUNDS:
                transpose_round(i)
                x_mx[i] = quantise_round(x_grouped[i], "x")
            if i == 0:
                prepare_wo()
            if 0 <= i - QUANTISE_H_LAG < ROUNDS:
                h_mx[i - QUANTISE_H_LAG] = quantise_round(h_grouped[i - QUANTISE_H_LAG], "h")
            if 0 <= i - SECOND_MATMUL_LAG < ROUNDS:
                second_matmul_round(i - SECOND_MATMUL_LAG)
            if 0 <= i - FIRST_MATMUL_LAG < ROUNDS:
                first_matmul_round(i - FIRST_MATMUL_LAG)
            if 0 <= i - SECOND_MATMUL_LAG < ROUNDS:
                store_round(i - SECOND_MATMUL_LAG)
            if 0 <= i - FIRST_MATMUL_LAG < ROUNDS:
                gate_round(i - FIRST_MATMUL_LAG)
